import numpy as np
import ml_dtypes


def mxq(x, axis, fmt="e4m3"):
    dtype, down = {"e4m3": (ml_dtypes.float8_e4m3fn, 7), "e5m2": (ml_dtypes.float8_e5m2, 14)}[fmt]
    v = np.moveaxis(np.asarray(x, np.float32).astype(ml_dtypes.bfloat16).astype(np.float64), axis, -1)
    blocks = v.reshape(v.shape[:-1] + (-1, 32))
    amax = np.abs(blocks).max(-1, keepdims=True)
    byte = np.maximum(np.where(amax > 0, np.frexp(amax)[1] - 1 + 127, 0) - down, 1)
    scale = np.exp2(byte - 127.0)
    codes = (blocks / scale).astype(np.float32).astype(dtype).astype(np.float64)
    return np.moveaxis((codes * scale).reshape(v.shape), -1, axis)


WIDE = False


def mx_kscale(k):
    if not WIDE:
        return np.ones(k)
    levels = np.array([20, -20, 10, -10, 0])
    a = np.random.permutation(np.resize(levels, k // 512 * 4)).reshape(k // 512, 4)
    idx = np.arange(k)
    return np.exp2(a[idx // 512, idx % 128 // 32])


BF16 = ml_dtypes.bfloat16


def bf(x):
    return np.asarray(x, np.float32).astype(BF16)


def f64(x):
    return np.asarray(x).astype(np.float64)


B, I, H = 1024, 1024, 1024
EPS = 1e-5


def ln(v):
    mu = v.mean(-1, keepdims=True)
    var = np.square(v - mu).mean(-1, keepdims=True)
    return (v - mu) / np.sqrt(var + EPS)


def sigmoid(v):
    return 1.0 / (1.0 + np.exp(-v))


def setup_inputs():
    s = mx_kscale(B)[:, None]
    x0 = bf(np.random.standard_normal((B, I)))
    h = bf(np.random.standard_normal((B, H)))
    r = bf(sigmoid(np.sqrt(2.0) * np.random.standard_normal((B, H))))
    z = bf(sigmoid(np.sqrt(2.0) * np.random.standard_normal((B, H))))
    W_in = bf(np.random.standard_normal((H, I)) / np.sqrt(I))
    b_in = bf(np.random.standard_normal(H) * 0.5)
    W_hn = bf(np.random.standard_normal((H, H)) / np.sqrt(H))
    b_hn = bf(np.random.standard_normal(H) * 0.5)
    g = bf(np.random.standard_normal((B, H)) * np.exp2(np.random.randint(-12, 1, (B, 1))) / s)
    a = f64(x0) @ f64(W_in).T + f64(b_in)
    mu = a.mean(-1, keepdims=True)
    var = np.square(a - mu).mean(-1, keepdims=True)
    rstd = 1.0 / np.sqrt(var + EPS)
    i_n = (a - mu) * rstd
    h_n = ln(f64(h) @ f64(W_hn).T + f64(b_hn))
    n = np.tanh(i_n + f64(r) * h_n)
    return {"x": bf(f64(x0) * s), "h": h, "r": r, "z": z,
            "W_in": W_in, "b_in": b_in, "W_hn": W_hn, "b_hn": b_hn,
            "n": np.asarray(n, np.float32),
            "i_n": np.asarray(i_n, np.float32),
            "rstd_in": np.asarray(rstd, np.float32),
            "grad_out": g}


def reference(x, h, r, z, W_in, b_in, W_hn, b_hn, n, i_n, rstd_in, grad_out):
    nf, inf_, rs = f64(n), f64(i_n), f64(rstd_in)
    di = f64(grad_out) * (1.0 - f64(z)) * (1.0 - nf * nf)
    m1 = di.mean(-1, keepdims=True)
    m2 = (di * inf_).mean(-1, keepdims=True)
    da = rs * (di - m1 - inf_ * m2)
    return mxq(da, 0, "e5m2").T @ mxq(f64(x), 0, "e4m3")

@@ -1,0 +1,158 @@
+from contextlib import ExitStack
+
+from concourse import mybir
+
+F32 = mybir.dt.float32
+BF16 = mybir.dt.bfloat16
+U32 = mybir.dt.uint32
+U8 = mybir.dt.uint8
+E4M3X4 = mybir.dt.float8_e4m3fn_x4
+E5M2X4 = mybir.dt.float8_e5m2_x4
+ALU = mybir.AluOpType
+ACT = mybir.ActivationFunctionType
+
+P = 128
+PACK = 4
+TOKENS = 1024
+PASSES = TOKENS // (P * PACK)
+H = 1024
+I = 1024
+M_TILE = 128
+N_TILE = 512
+X_PIECE = I // PACK
+RUN = 4
+
+FLOPS = 2 * TOKENS * H * I
+BYTES = 3 * TOKENS * H * 2 + 2 * TOKENS * H * 4 + TOKENS * 4 + H * I * 4
+
+
+def rows_to_words(rows):
+    return rows.rearrange("p t (c i) -> p c t i", i=RUN)
+
+
+def words_as_written(grouped):
+    return grouped.rearrange("p (c i) t -> p c t i", i=RUN)
+
+
+def tile_layernormgrucell_pb_v_kernel(
+    tc, x, h, r, z, W_in, b_in, W_hn, b_hn, n, i_n, rstd_in, grad_out, out
+):
+    nc = tc.nc
+
+    def chunks(dram):
+        return dram.rearrange("(c p t) w -> c p t w", p=P, t=PACK)
+
+    x_view, z_view, n_view, i_view, g_view = (chunks(a) for a in (x, z, n, i_n, grad_out))
+
+    with ExitStack() as ctx:
+        keep = ctx.enter_context(tc.tile_pool(name="keep", bufs=1))
+        loads = ctx.enter_context(tc.tile_pool(name="loads", bufs=4))
+        work = ctx.enter_context(tc.tile_pool(name="work", bufs=2))
+        stats = ctx.enter_context(tc.tile_pool(name="stats", bufs=PASSES * PACK))
+        psum = ctx.enter_context(tc.psum_pool(name="psum", bufs=8))
+
+        x_codes = keep.tile([P, PASSES, I], U32, align_bytes=64)
+        x_scales = keep.tile([P, PASSES, I], U8, align_bytes=64)
+        da_codes = keep.tile([P, PASSES, H], U32, align_bytes=64)
+        da_scales = keep.tile([P, PASSES, H], U8, align_bytes=64)
+
+        rstd = keep.tile([P, PASSES, PACK], F32)
+        nc.sync.dma_start(
+            out=rstd[:], in_=rstd_in.rearrange("(c p t) o -> p c (t o)", p=P, t=PACK)
+        )
+
+        def da_block(c, m, e_rows, corr_rows):
+            m_cols = slice(m * M_TILE, (m + 1) * M_TILE)
+            da_grouped = work.tile([P, M_TILE, PACK], BF16, align_bytes=64, bufs=4)
+            nc.vector.tensor_tensor(
+                out=words_as_written(da_grouped[:]),
+                in0=rows_to_words(e_rows[:, :, m_cols]),
+                in1=rows_to_words(corr_rows[:, :, m_cols]),
+                op=ALU.add,
+            )
+            nc.vector.quantize_mx(
+                out=da_codes[:, c, m_cols].bitcast(E5M2X4),
+                scales=da_scales[:, c, m_cols],
+                in_=da_grouped[:].rearrange("p w t -> p (w t)"),
+            )
+
+        pass_rows = []
+        for c in range(PASSES):
+            x_rows = work.tile([P, PACK, I], BF16)
+            e_rows = work.tile([P, PACK, H], F32)
+            corr_rows = work.tile([P, PACK, H], F32)
+            pass_rows.append((e_rows, corr_rows))
+            for t in range(PACK):
+                g_row = loads.tile([P, H], BF16)
+                z_row = loads.tile([P, H], BF16)
+                n_row = loads.tile([P, H], F32)
+                i_row = loads.tile([P, H], F32)
+                nc.sync.dma_start(out=g_row[:], in_=g_view[c][:, t, :])
+                nc.sync.dma_start(out=z_row[:], in_=z_view[c][:, t, :])
+                nc.sync.dma_start(out=n_row[:], in_=n_view[c][:, t, :])
+                nc.sync.dma_start(out=i_row[:], in_=i_view[c][:, t, :])
+                if t == 1:
+                    nc.sync.dma_start(out=x_rows[:], in_=x_view[c])
+
+                g_scaled = work.tile([P, H], F32)
+                nc.scalar.activation(
+                    out=g_scaled[:], in_=g_row[:], func=ACT.Copy, scale=rstd[:, c, t : t + 1]
+                )
+                n_squared = work.tile([P, H], F32)
+                nc.scalar.activation(out=n_squared[:], in_=n_row[:], func=ACT.Square)
+
+                blend = work.tile([P, H], F32)
+                nc.vector.scalar_tensor_tensor(
+                    out=blend[:], in0=z_row[:], scalar=1.0, in1=g_scaled[:],
+                    op0=ALU.subtract, op1=ALU.mult,
+                )
+                sum_e = stats.tile([P, 1], F32)
+                nc.vector.scalar_tensor_tensor(
+                    out=e_rows[:, t, :], in0=n_squared[:], scalar=1.0, in1=blend[:],
+                    op0=ALU.subtract, op1=ALU.mult, accum_out=sum_e[:],
+                )
+                products = work.tile([P, H], F32)
+                neg_m2 = stats.tile([P, 1], F32)
+                nc.vector.scalar_tensor_tensor(
+                    out=products[:], in0=e_rows[:, t, :], scalar=-1.0 / H, in1=i_row[:],
+                    op0=ALU.mult, op1=ALU.mult, accum_out=neg_m2[:],
+                )
+                neg_m1 = stats.tile([P, 1], F32)
+                nc.scalar.mul(out=neg_m1[:], in_=sum_e[:], mul=-1.0 / H)
+                nc.scalar.activation(
+                    out=corr_rows[:, t, :], in_=i_row[:], func=ACT.Identity,
+                    scale=neg_m2[:, 0:1], bias=neg_m1[:, 0:1],
+                )
+
+            for piece in range(PACK):
+                x_cols = slice(piece * X_PIECE, (piece + 1) * X_PIECE)
+                x_grouped = work.tile([P, X_PIECE, PACK], BF16, align_bytes=64, bufs=3)
+                nc.scalar.copy(
+                    out=words_as_written(x_grouped[:]), in_=rows_to_words(x_rows[:, :, x_cols])
+                )
+                nc.vector.quantize_mx(
+                    out=x_codes[:, c, x_cols].bitcast(E4M3X4),
+                    scales=x_scales[:, c, x_cols],
+                    in_=x_grouped[:].rearrange("p w t -> p (w t)"),
+                )
+
+        for m in range(H // M_TILE):
+            m_cols = slice(m * M_TILE, (m + 1) * M_TILE)
+            for c in range(PASSES):
+                da_block(c, m, *pass_rows[c])
+            out_rows = work.tile([P, I], F32, bufs=4)
+            for nt in range(I // N_TILE):
+                n_cols = slice(nt * N_TILE, (nt + 1) * N_TILE)
+                acc = psum.tile([M_TILE, N_TILE], F32)
+                for c in range(PASSES):
+                    nc.tensor.matmul_mx(
+                        out=acc[:],
+                        lhsT=da_codes[:, c, m_cols].bitcast(E5M2X4),
+                        lhsT_scale=da_scales[:, c, m_cols],
+                        rhs=x_codes[:, c, n_cols].bitcast(E4M3X4),
+                        rhs_scale=x_scales[:, c, n_cols],
+                        start=(c == 0),
+                        stop=(c == PASSES - 1),
+                    )
+                nc.scalar.copy(out=out_rows[:, n_cols], in_=acc[:])
+            nc.sync.dma_start(out=out[m_cols, :], in_=out_rows[:])

@@ -15,12 +15,17 @@ P = 128
 PACK = 4
 TOKENS = 1024
 PASSES = TOKENS // (P * PACK)
+CHUNKS = PASSES * PACK
 H = 1024
 I = 1024
 M_TILE = 128
+M_TILES = H // M_TILE
 N_TILE = 512
+N_TILES = I // N_TILE
 X_PIECE = I // PACK
 RUN = 4
+AHEAD = 3
+EARLY = PACK
 
 FLOPS = 2 * TOKENS * H * I
 BYTES = 3 * TOKENS * H * 2 + 2 * TOKENS * H * 4 + TOKENS * 4 + H * I * 4
@@ -45,10 +50,11 @@ def tile_layernormgrucell_pb_v_kernel(
     x_view, z_view, n_view, i_view, g_view = (chunks(a) for a in (x, z, n, i_n, grad_out))
 
     with ExitStack() as ctx:
+        ctx.enter_context(tc.manual_schedule())
         keep = ctx.enter_context(tc.tile_pool(name="keep", bufs=1))
-        loads = ctx.enter_context(tc.tile_pool(name="loads", bufs=4))
+        loads = ctx.enter_context(tc.tile_pool(name="loads", bufs=AHEAD + 1))
         work = ctx.enter_context(tc.tile_pool(name="work", bufs=2))
-        stats = ctx.enter_context(tc.tile_pool(name="stats", bufs=PASSES * PACK))
+        stats = ctx.enter_context(tc.tile_pool(name="stats", bufs=CHUNKS))
         psum = ctx.enter_context(tc.psum_pool(name="psum", bufs=8))
 
         x_codes = keep.tile([P, PASSES, I], U32, align_bytes=64)
@@ -56,103 +62,183 @@ def tile_layernormgrucell_pb_v_kernel(
         da_codes = keep.tile([P, PASSES, H], U32, align_bytes=64)
         da_scales = keep.tile([P, PASSES, H], U8, align_bytes=64)
 
-        rstd = keep.tile([P, PASSES, PACK], F32)
+        rstd = keep.tile([P, CHUNKS], F32)
         nc.sync.dma_start(
-            out=rstd[:], in_=rstd_in.rearrange("(c p t) o -> p c (t o)", p=P, t=PACK)
+            out=rstd[:].rearrange("p (c t) -> p c t", t=PACK),
+            in_=rstd_in.rearrange("(c p t) o -> p c (t o)", p=P, t=PACK),
         )
+        guess = keep.tile([P, CHUNKS], F32)
+        nc.scalar.activation(out=guess[:], in_=rstd[:], func=ACT.Sqrt)
+        inverse = keep.tile([P, CHUNKS], F32)
+        nc.vector.reciprocal(out=inverse[:], in_=guess[:])
+        half_quotient = keep.tile([P, CHUNKS], F32)
+        nc.vector.scalar_tensor_tensor(
+            out=half_quotient[:], in0=rstd[:], scalar=0.5, in1=inverse[:],
+            op0=ALU.mult, op1=ALU.mult,
+        )
+        root = keep.tile([P, CHUNKS], F32)
+        nc.vector.scalar_tensor_tensor(
+            out=root[:], in0=guess[:], scalar=0.5, in1=half_quotient[:],
+            op0=ALU.mult, op1=ALU.add,
+        )
+        root_squared = keep.tile([P, CHUNKS], F32)
+        nc.vector.tensor_tensor(out=root_squared[:], in0=root[:], in1=root[:], op=ALU.mult)
 
-        def da_block(c, m, e_rows, corr_rows):
+        rows = {}
+        x_rows = {}
+        e_rows = {}
+        corr_rows = {}
+        n_squared = {}
+        blend = {}
+        neg_means = {}
+        x_grouped = {}
+        da_grouped = {}
+        acc = {}
+
+        def load_chunk(k):
+            c, t = divmod(k, PACK)
+            for name, view, dtype in (
+                ("n", n_view, F32), ("g", g_view, BF16), ("z", z_view, BF16), ("i", i_view, F32)
+            ):
+                rows[name, k] = loads.tile([P, H], dtype, name=name + "_row")
+                nc.sync.dma_start(out=rows[name, k][:], in_=view[c][:, t, :])
+            if t == 1:
+                x_rows[c] = work.tile([P, PACK, I], BF16, name="x_rows")
+                nc.sync.dma_start(out=x_rows[c][:], in_=x_view[c])
+
+        def square(k):
+            n_squared[k] = work.tile([P, H], F32, name="n_squared")
+            nc.scalar.activation(
+                out=n_squared[k][:], in_=rows["n", k][:], func=ACT.Square,
+                scale=root[:, k : k + 1],
+            )
+
+        def blend_gate(k):
+            blend[k] = work.tile([P, H], F32, name="blend")
+            nc.vector.scalar_tensor_tensor(
+                out=blend[k][:], in0=rows["z", k][:], scalar=1.0, in1=rows["g", k][:],
+                op0=ALU.subtract, op1=ALU.mult,
+            )
+
+        def gradient(k):
+            c, t = divmod(k, PACK)
+            if t == 0:
+                e_rows[c] = work.tile([P, PACK, H], F32, name="e_rows")
+                corr_rows[c] = work.tile([P, PACK, H], F32, name="corr_rows")
+            sum_e = stats.tile([P, 1], F32)
+            nc.vector.scalar_tensor_tensor(
+                out=e_rows[c][:, t, :], in0=n_squared[k][:], scalar=root_squared[:, k : k + 1],
+                in1=blend[k][:], op0=ALU.subtract, op1=ALU.mult, accum_out=sum_e[:],
+            )
+            products = work.tile([P, H], F32)
+            neg_m2 = stats.tile([P, 1], F32)
+            nc.vector.scalar_tensor_tensor(
+                out=products[:], in0=e_rows[c][:, t, :], scalar=-1.0 / H, in1=rows["i", k][:],
+                op0=ALU.mult, op1=ALU.mult, accum_out=neg_m2[:],
+            )
+            neg_means[k] = (sum_e, neg_m2)
+
+        def correction(k):
+            c, t = divmod(k, PACK)
+            sum_e, neg_m2 = neg_means[k]
+            neg_m1 = stats.tile([P, 1], F32)
+            nc.scalar.mul(out=neg_m1[:], in_=sum_e[:], mul=-1.0 / H)
+            nc.scalar.activation(
+                out=corr_rows[c][:, t, :], in_=rows["i", k][:], func=ACT.Identity,
+                scale=neg_m2[:, 0:1], bias=neg_m1[:, 0:1],
+            )
+
+        def regroup_x(piece):
+            c, quarter = divmod(piece, PACK)
+            x_cols = slice(quarter * X_PIECE, (quarter + 1) * X_PIECE)
+            x_grouped[piece] = work.tile(
+                [P, X_PIECE, PACK], BF16, align_bytes=64, bufs=4, name="x_grouped"
+            )
+            nc.scalar.copy(
+                out=words_as_written(x_grouped[piece][:]),
+                in_=rows_to_words(x_rows[c][:, :, x_cols]),
+            )
+
+        def quantise_x(piece):
+            c, quarter = divmod(piece, PACK)
+            x_cols = slice(quarter * X_PIECE, (quarter + 1) * X_PIECE)
+            nc.vector.quantize_mx(
+                out=x_codes[:, c, x_cols].bitcast(E4M3X4),
+                scales=x_scales[:, c, x_cols],
+                in_=x_grouped[piece][:].rearrange("p w t -> p (w t)"),
+            )
+
+        def add_da(c, m):
             m_cols = slice(m * M_TILE, (m + 1) * M_TILE)
-            da_grouped = work.tile([P, M_TILE, PACK], BF16, align_bytes=64, bufs=4)
+            da_grouped[c, m] = work.tile(
+                [P, M_TILE, PACK], BF16, align_bytes=64, bufs=4, name="da_grouped"
+            )
             nc.vector.tensor_tensor(
-                out=words_as_written(da_grouped[:]),
-                in0=rows_to_words(e_rows[:, :, m_cols]),
-                in1=rows_to_words(corr_rows[:, :, m_cols]),
+                out=words_as_written(da_grouped[c, m][:]),
+                in0=rows_to_words(e_rows[c][:, :, m_cols]),
+                in1=rows_to_words(corr_rows[c][:, :, m_cols]),
                 op=ALU.add,
             )
+
+        def quantise_da_and_multiply(c, m):
+            m_cols = slice(m * M_TILE, (m + 1) * M_TILE)
             nc.vector.quantize_mx(
                 out=da_codes[:, c, m_cols].bitcast(E5M2X4),
                 scales=da_scales[:, c, m_cols],
-                in_=da_grouped[:].rearrange("p w t -> p (w t)"),
+                in_=da_grouped[c, m][:].rearrange("p w t -> p (w t)"),
             )
-
-        pass_rows = []
-        for c in range(PASSES):
-            x_rows = work.tile([P, PACK, I], BF16)
-            e_rows = work.tile([P, PACK, H], F32)
-            corr_rows = work.tile([P, PACK, H], F32)
-            pass_rows.append((e_rows, corr_rows))
-            for t in range(PACK):
-                g_row = loads.tile([P, H], BF16)
-                z_row = loads.tile([P, H], BF16)
-                n_row = loads.tile([P, H], F32)
-                i_row = loads.tile([P, H], F32)
-                nc.sync.dma_start(out=g_row[:], in_=g_view[c][:, t, :])
-                nc.sync.dma_start(out=z_row[:], in_=z_view[c][:, t, :])
-                nc.sync.dma_start(out=n_row[:], in_=n_view[c][:, t, :])
-                nc.sync.dma_start(out=i_row[:], in_=i_view[c][:, t, :])
-                if t == 1:
-                    nc.sync.dma_start(out=x_rows[:], in_=x_view[c])
-
-                g_scaled = work.tile([P, H], F32)
-                nc.scalar.activation(
-                    out=g_scaled[:], in_=g_row[:], func=ACT.Copy, scale=rstd[:, c, t : t + 1]
-                )
-                n_squared = work.tile([P, H], F32)
-                nc.scalar.activation(out=n_squared[:], in_=n_row[:], func=ACT.Square)
-
-                blend = work.tile([P, H], F32)
-                nc.vector.scalar_tensor_tensor(
-                    out=blend[:], in0=z_row[:], scalar=1.0, in1=g_scaled[:],
-                    op0=ALU.subtract, op1=ALU.mult,
-                )
-                sum_e = stats.tile([P, 1], F32)
-                nc.vector.scalar_tensor_tensor(
-                    out=e_rows[:, t, :], in0=n_squared[:], scalar=1.0, in1=blend[:],
-                    op0=ALU.subtract, op1=ALU.mult, accum_out=sum_e[:],
-                )
-                products = work.tile([P, H], F32)
-                neg_m2 = stats.tile([P, 1], F32)
-                nc.vector.scalar_tensor_tensor(
-                    out=products[:], in0=e_rows[:, t, :], scalar=-1.0 / H, in1=i_row[:],
-                    op0=ALU.mult, op1=ALU.mult, accum_out=neg_m2[:],
-                )
-                neg_m1 = stats.tile([P, 1], F32)
-                nc.scalar.mul(out=neg_m1[:], in_=sum_e[:], mul=-1.0 / H)
-                nc.scalar.activation(
-                    out=corr_rows[:, t, :], in_=i_row[:], func=ACT.Identity,
-                    scale=neg_m2[:, 0:1], bias=neg_m1[:, 0:1],
-                )
-
-            for piece in range(PACK):
-                x_cols = slice(piece * X_PIECE, (piece + 1) * X_PIECE)
-                x_grouped = work.tile([P, X_PIECE, PACK], BF16, align_bytes=64, bufs=3)
-                nc.scalar.copy(
-                    out=words_as_written(x_grouped[:]), in_=rows_to_words(x_rows[:, :, x_cols])
-                )
-                nc.vector.quantize_mx(
-                    out=x_codes[:, c, x_cols].bitcast(E4M3X4),
-                    scales=x_scales[:, c, x_cols],
-                    in_=x_grouped[:].rearrange("p w t -> p (w t)"),
-                )
-
-        for m in range(H // M_TILE):
-            m_cols = slice(m * M_TILE, (m + 1) * M_TILE)
-            for c in range(PASSES):
-                da_block(c, m, *pass_rows[c])
-            out_rows = work.tile([P, I], F32, bufs=4)
-            for nt in range(I // N_TILE):
+            for nt in range(N_TILES):
                 n_cols = slice(nt * N_TILE, (nt + 1) * N_TILE)
-                acc = psum.tile([M_TILE, N_TILE], F32)
-                for c in range(PASSES):
-                    nc.tensor.matmul_mx(
-                        out=acc[:],
-                        lhsT=da_codes[:, c, m_cols].bitcast(E5M2X4),
-                        lhsT_scale=da_scales[:, c, m_cols],
-                        rhs=x_codes[:, c, n_cols].bitcast(E4M3X4),
-                        rhs_scale=x_scales[:, c, n_cols],
-                        start=(c == 0),
-                        stop=(c == PASSES - 1),
-                    )
-                nc.scalar.copy(out=out_rows[:, n_cols], in_=acc[:])
-            nc.sync.dma_start(out=out[m_cols, :], in_=out_rows[:])
+                if c == 0:
+                    acc[m, nt] = psum.tile([M_TILE, N_TILE], F32, name="acc")
+                nc.tensor.matmul_mx(
+                    out=acc[m, nt][:],
+                    lhsT=da_codes[:, c, m_cols].bitcast(E5M2X4),
+                    lhsT_scale=da_scales[:, c, m_cols],
+                    rhs=x_codes[:, c, n_cols].bitcast(E4M3X4),
+                    rhs_scale=x_scales[:, c, n_cols],
+                    start=(c == 0),
+                    stop=(c == PASSES - 1),
+                )
+
+        def store_rows(m):
+            out_rows = work.tile([P, I], F32, bufs=4)
+            for nt in range(N_TILES):
+                nc.scalar.copy(out=out_rows[:, nt * N_TILE : (nt + 1) * N_TILE], in_=acc[m, nt][:])
+            nc.sync.dma_start(out=out[m * M_TILE : (m + 1) * M_TILE, :], in_=out_rows[:])
+
+        for k in range(AHEAD):
+            load_chunk(k)
+        square(0)
+        for k in range(CHUNKS):
+            if k + AHEAD < CHUNKS:
+                load_chunk(k + AHEAD)
+            if k + 1 < CHUNKS:
+                square(k + 1)
+            else:
+                regroup_x(CHUNKS - 1)
+            blend_gate(k)
+            if k >= 2:
+                quantise_x(k - 2)
+            if k > PACK:
+                quantise_da_and_multiply(0, k - PACK - 1)
+            gradient(k)
+            if k >= 1:
+                regroup_x(k - 1)
+            correction(k)
+            if k >= PACK:
+                add_da(0, k - PACK)
+        quantise_x(CHUNKS - 2)
+        quantise_x(CHUNKS - 1)
+        quantise_da_and_multiply(0, EARLY - 1)
+
+        todo = [(1, m) for m in range(EARLY)]
+        todo += [(c, m) for m in range(EARLY, M_TILES) for c in range(PASSES)]
+        for step in range(len(todo) + 1):
+            if step < len(todo):
+                add_da(*todo[step])
+            if step >= 1:
+                c, m = todo[step - 1]
+                quantise_da_and_multiply(c, m)
+                if c == PASSES - 1:
+                    store_rows(m)

@@ -90,7 +90,9 @@ def tile_layernormgrucell_pb_v_kernel(
         corr_rows = {}
         n_squared = {}
         blend = {}
-        neg_means = {}
+        sum_e = {}
+        neg_m1 = {}
+        neg_m2 = {}
         x_grouped = {}
         da_grouped = {}
         acc = {}
@@ -125,27 +127,27 @@ def tile_layernormgrucell_pb_v_kernel(
             if t == 0:
                 e_rows[c] = work.tile([P, PACK, H], F32, name="e_rows")
                 corr_rows[c] = work.tile([P, PACK, H], F32, name="corr_rows")
-            sum_e = stats.tile([P, 1], F32)
+            sum_e[k] = stats.tile([P, 1], F32, name="sum_e")
             nc.vector.scalar_tensor_tensor(
                 out=e_rows[c][:, t, :], in0=n_squared[k][:], scalar=root_squared[:, k : k + 1],
-                in1=blend[k][:], op0=ALU.subtract, op1=ALU.mult, accum_out=sum_e[:],
+                in1=blend[k][:], op0=ALU.subtract, op1=ALU.mult, accum_out=sum_e[k][:],
             )
             products = work.tile([P, H], F32)
-            neg_m2 = stats.tile([P, 1], F32)
+            neg_m2[k] = stats.tile([P, 1], F32, name="neg_m2")
             nc.vector.scalar_tensor_tensor(
                 out=products[:], in0=e_rows[c][:, t, :], scalar=-1.0 / H, in1=rows["i", k][:],
-                op0=ALU.mult, op1=ALU.mult, accum_out=neg_m2[:],
+                op0=ALU.mult, op1=ALU.mult, accum_out=neg_m2[k][:],
             )
-            neg_means[k] = (sum_e, neg_m2)
+
+        def negative_mean(k):
+            neg_m1[k] = stats.tile([P, 1], F32, name="neg_m1")
+            nc.scalar.mul(out=neg_m1[k][:], in_=sum_e[k][:], mul=-1.0 / H)
 
         def correction(k):
             c, t = divmod(k, PACK)
-            sum_e, neg_m2 = neg_means[k]
-            neg_m1 = stats.tile([P, 1], F32)
-            nc.scalar.mul(out=neg_m1[:], in_=sum_e[:], mul=-1.0 / H)
             nc.scalar.activation(
                 out=corr_rows[c][:, t, :], in_=rows["i", k][:], func=ACT.Identity,
-                scale=neg_m2[:, 0:1], bias=neg_m1[:, 0:1],
+                scale=neg_m2[k][:, 0:1], bias=neg_m1[k][:, 0:1],
             )
 
         def regroup_x(piece):
@@ -202,10 +204,13 @@ def tile_layernormgrucell_pb_v_kernel(
                 )
 
         def store_rows(m):
-            out_rows = work.tile([P, I], F32, bufs=4)
             for nt in range(N_TILES):
-                nc.scalar.copy(out=out_rows[:, nt * N_TILE : (nt + 1) * N_TILE], in_=acc[m, nt][:])
-            nc.sync.dma_start(out=out[m * M_TILE : (m + 1) * M_TILE, :], in_=out_rows[:])
+                out_part = work.tile([P, N_TILE], F32, bufs=8)
+                nc.scalar.copy(out=out_part[:], in_=acc[m, nt][:])
+                nc.sync.dma_start(
+                    out=out[m * M_TILE : (m + 1) * M_TILE, nt * N_TILE : (nt + 1) * N_TILE],
+                    in_=out_part[:],
+                )
 
         for k in range(AHEAD):
             load_chunk(k)
@@ -223,6 +228,7 @@ def tile_layernormgrucell_pb_v_kernel(
             if k > PACK:
                 quantise_da_and_multiply(0, k - PACK - 1)
             gradient(k)
+            negative_mean(k)
             if k >= 1:
                 regroup_x(k - 1)
             correction(k)

@@ -23,6 +23,7 @@ M_TILES = H // M_TILE
 N_TILE = 512
 N_TILES = I // N_TILE
 X_PIECE = I // PACK
+X_HALF = X_PIECE // 2
 RUN = 4
 AHEAD = 3
 EARLY = PACK
@@ -132,6 +133,9 @@ def tile_layernormgrucell_pb_v_kernel(
                 out=e_rows[c][:, t, :], in0=n_squared[k][:], scalar=root_squared[:, k : k + 1],
                 in1=blend[k][:], op0=ALU.subtract, op1=ALU.mult, accum_out=sum_e[k][:],
             )
+
+        def mean_with_i_n(k):
+            c, t = divmod(k, PACK)
             products = work.tile([P, H], F32)
             neg_m2[k] = stats.tile([P, 1], F32, name="neg_m2")
             nc.vector.scalar_tensor_tensor(
@@ -161,13 +165,14 @@ def tile_layernormgrucell_pb_v_kernel(
                 in_=rows_to_words(x_rows[c][:, :, x_cols]),
             )
 
-        def quantise_x(piece):
+        def quantise_x(piece, half):
             c, quarter = divmod(piece, PACK)
-            x_cols = slice(quarter * X_PIECE, (quarter + 1) * X_PIECE)
+            half_cols = slice(half * X_HALF, (half + 1) * X_HALF)
+            x_cols = slice(quarter * X_PIECE + half * X_HALF, quarter * X_PIECE + (half + 1) * X_HALF)
             nc.vector.quantize_mx(
                 out=x_codes[:, c, x_cols].bitcast(E4M3X4),
                 scales=x_scales[:, c, x_cols],
-                in_=x_grouped[piece][:].rearrange("p w t -> p (w t)"),
+                in_=x_grouped[piece][:, half_cols, :].rearrange("p w t -> p (w t)"),
             )
 
         def add_da(c, m):
@@ -224,18 +229,22 @@ def tile_layernormgrucell_pb_v_kernel(
                 regroup_x(CHUNKS - 1)
             blend_gate(k)
             if k >= 2:
-                quantise_x(k - 2)
+                quantise_x(k - 2, 0)
+            gradient(k)
+            if k >= 2:
+                quantise_x(k - 2, 1)
             if k > PACK:
                 quantise_da_and_multiply(0, k - PACK - 1)
-            gradient(k)
+            mean_with_i_n(k)
             negative_mean(k)
             if k >= 1:
                 regroup_x(k - 1)
             correction(k)
             if k >= PACK:
                 add_da(0, k - PACK)
-        quantise_x(CHUNKS - 2)
-        quantise_x(CHUNKS - 1)
+        for piece in (CHUNKS - 2, CHUNKS - 1):
+            for half in range(2):
+                quantise_x(piece, half)
         quantise_da_and_multiply(0, EARLY - 1)
 
         todo = [(1, m) for m in range(EARLY)]

from contextlib import ExitStack

from concourse import mybir

F32 = mybir.dt.float32
BF16 = mybir.dt.bfloat16
U32 = mybir.dt.uint32
U8 = mybir.dt.uint8
E4M3X4 = mybir.dt.float8_e4m3fn_x4
E5M2X4 = mybir.dt.float8_e5m2_x4
ALU = mybir.AluOpType
ACT = mybir.ActivationFunctionType

P = 128
PACK = 4
TOKENS = 1024
PASSES = TOKENS // (P * PACK)
CHUNKS = PASSES * PACK
H = 1024
I = 1024
M_TILE = 128
M_TILES = H // M_TILE
N_TILE = 512
N_TILES = I // N_TILE
X_PIECE = I // PACK
X_HALF = X_PIECE // 2
RUN = 4
AHEAD = 3
EARLY = PACK

FLOPS = 2 * TOKENS * H * I
BYTES = 3 * TOKENS * H * 2 + 2 * TOKENS * H * 4 + TOKENS * 4 + H * I * 4


def rows_to_words(rows):
    return rows.rearrange("p t (c i) -> p c t i", i=RUN)


def words_as_written(grouped):
    return grouped.rearrange("p (c i) t -> p c t i", i=RUN)


def tile_layernormgrucell_pb_v_kernel(
    tc, x, h, r, z, W_in, b_in, W_hn, b_hn, n, i_n, rstd_in, grad_out, out
):
    nc = tc.nc

    def chunks(dram):
        return dram.rearrange("(c p t) w -> c p t w", p=P, t=PACK)

    x_view, z_view, n_view, i_view, g_view = (chunks(a) for a in (x, z, n, i_n, grad_out))

    with ExitStack() as ctx:
        ctx.enter_context(tc.manual_schedule())
        keep = ctx.enter_context(tc.tile_pool(name="keep", bufs=1))
        loads = ctx.enter_context(tc.tile_pool(name="loads", bufs=AHEAD + 1))
        work = ctx.enter_context(tc.tile_pool(name="work", bufs=2))
        stats = ctx.enter_context(tc.tile_pool(name="stats", bufs=CHUNKS))
        psum = ctx.enter_context(tc.psum_pool(name="psum", bufs=8))

        x_codes = keep.tile([P, PASSES, I], U32, align_bytes=64)
        x_scales = keep.tile([P, PASSES, I], U8, align_bytes=64)
        da_codes = keep.tile([P, PASSES, H], U32, align_bytes=64)
        da_scales = keep.tile([P, PASSES, H], U8, align_bytes=64)

        rstd = keep.tile([P, CHUNKS], F32)
        nc.sync.dma_start(
            out=rstd[:].rearrange("p (c t) -> p c t", t=PACK),
            in_=rstd_in.rearrange("(c p t) o -> p c (t o)", p=P, t=PACK),
        )
        guess = keep.tile([P, CHUNKS], F32)
        nc.scalar.activation(out=guess[:], in_=rstd[:], func=ACT.Sqrt)
        inverse = keep.tile([P, CHUNKS], F32)
        nc.vector.reciprocal(out=inverse[:], in_=guess[:])
        half_quotient = keep.tile([P, CHUNKS], F32)
        nc.vector.scalar_tensor_tensor(
            out=half_quotient[:], in0=rstd[:], scalar=0.5, in1=inverse[:],
            op0=ALU.mult, op1=ALU.mult,
        )
        root = keep.tile([P, CHUNKS], F32)
        nc.vector.scalar_tensor_tensor(
            out=root[:], in0=guess[:], scalar=0.5, in1=half_quotient[:],
            op0=ALU.mult, op1=ALU.add,
        )
        root_squared = keep.tile([P, CHUNKS], F32)
        nc.vector.tensor_tensor(out=root_squared[:], in0=root[:], in1=root[:], op=ALU.mult)

        rows = {}
        x_rows = {}
        e_rows = {}
        corr_rows = {}
        n_squared = {}
        blend = {}
        sum_e = {}
        neg_m1 = {}
        neg_m2 = {}
        x_grouped = {}
        da_grouped = {}
        acc = {}

        def load_chunk(k):
            c, t = divmod(k, PACK)
            for name, view, dtype in (
                ("n", n_view, F32), ("g", g_view, BF16), ("z", z_view, BF16), ("i", i_view, F32)
            ):
                rows[name, k] = loads.tile([P, H], dtype, name=name + "_row")
                nc.sync.dma_start(out=rows[name, k][:], in_=view[c][:, t, :])
            if t == 1:
                x_rows[c] = work.tile([P, PACK, I], BF16, name="x_rows")
                nc.sync.dma_start(out=x_rows[c][:], in_=x_view[c])

        def square(k):
            n_squared[k] = work.tile([P, H], F32, name="n_squared")
            nc.scalar.activation(
                out=n_squared[k][:], in_=rows["n", k][:], func=ACT.Square,
                scale=root[:, k : k + 1],
            )

        def blend_gate(k):
            blend[k] = work.tile([P, H], F32, name="blend")
            nc.vector.scalar_tensor_tensor(
                out=blend[k][:], in0=rows["z", k][:], scalar=1.0, in1=rows["g", k][:],
                op0=ALU.subtract, op1=ALU.mult,
            )

        def gradient(k):
            c, t = divmod(k, PACK)
            if t == 0:
                e_rows[c] = work.tile([P, PACK, H], F32, name="e_rows")
                corr_rows[c] = work.tile([P, PACK, H], F32, name="corr_rows")
            sum_e[k] = stats.tile([P, 1], F32, name="sum_e")
            nc.vector.scalar_tensor_tensor(
                out=e_rows[c][:, t, :], in0=n_squared[k][:], scalar=root_squared[:, k : k + 1],
                in1=blend[k][:], op0=ALU.subtract, op1=ALU.mult, accum_out=sum_e[k][:],
            )

        def mean_with_i_n(k):
            c, t = divmod(k, PACK)
            products = work.tile([P, H], F32)
            neg_m2[k] = stats.tile([P, 1], F32, name="neg_m2")
            nc.vector.scalar_tensor_tensor(
                out=products[:], in0=e_rows[c][:, t, :], scalar=-1.0 / H, in1=rows["i", k][:],
                op0=ALU.mult, op1=ALU.mult, accum_out=neg_m2[k][:],
            )

        def negative_mean(k):
            neg_m1[k] = stats.tile([P, 1], F32, name="neg_m1")
            nc.scalar.mul(out=neg_m1[k][:], in_=sum_e[k][:], mul=-1.0 / H)

        def correction(k):
            c, t = divmod(k, PACK)
            nc.scalar.activation(
                out=corr_rows[c][:, t, :], in_=rows["i", k][:], func=ACT.Identity,
                scale=neg_m2[k][:, 0:1], bias=neg_m1[k][:, 0:1],
            )

        def regroup_x(piece):
            c, quarter = divmod(piece, PACK)
            x_cols = slice(quarter * X_PIECE, (quarter + 1) * X_PIECE)
            x_grouped[piece] = work.tile(
                [P, X_PIECE, PACK], BF16, align_bytes=64, bufs=4, name="x_grouped"
            )
            nc.scalar.copy(
                out=words_as_written(x_grouped[piece][:]),
                in_=rows_to_words(x_rows[c][:, :, x_cols]),
            )

        def quantise_x(piece, half):
            c, quarter = divmod(piece, PACK)
            half_cols = slice(half * X_HALF, (half + 1) * X_HALF)
            x_cols = slice(quarter * X_PIECE + half * X_HALF, quarter * X_PIECE + (half + 1) * X_HALF)
            nc.vector.quantize_mx(
                out=x_codes[:, c, x_cols].bitcast(E4M3X4),
                scales=x_scales[:, c, x_cols],
                in_=x_grouped[piece][:, half_cols, :].rearrange("p w t -> p (w t)"),
            )

        def add_da(c, m):
            m_cols = slice(m * M_TILE, (m + 1) * M_TILE)
            da_grouped[c, m] = work.tile(
                [P, M_TILE, PACK], BF16, align_bytes=64, bufs=4, name="da_grouped"
            )
            nc.vector.tensor_tensor(
                out=words_as_written(da_grouped[c, m][:]),
                in0=rows_to_words(e_rows[c][:, :, m_cols]),
                in1=rows_to_words(corr_rows[c][:, :, m_cols]),
                op=ALU.add,
            )

        def quantise_da_and_multiply(c, m):
            m_cols = slice(m * M_TILE, (m + 1) * M_TILE)
            nc.vector.quantize_mx(
                out=da_codes[:, c, m_cols].bitcast(E5M2X4),
                scales=da_scales[:, c, m_cols],
                in_=da_grouped[c, m][:].rearrange("p w t -> p (w t)"),
            )
            for nt in range(N_TILES):
                n_cols = slice(nt * N_TILE, (nt + 1) * N_TILE)
                if c == 0:
                    acc[m, nt] = psum.tile([M_TILE, N_TILE], F32, name="acc")
                nc.tensor.matmul_mx(
                    out=acc[m, nt][:],
                    lhsT=da_codes[:, c, m_cols].bitcast(E5M2X4),
                    lhsT_scale=da_scales[:, c, m_cols],
                    rhs=x_codes[:, c, n_cols].bitcast(E4M3X4),
                    rhs_scale=x_scales[:, c, n_cols],
                    start=(c == 0),
                    stop=(c == PASSES - 1),
                )

        def store_rows(m):
            for nt in range(N_TILES):
                out_part = work.tile([P, N_TILE], F32, bufs=8)
                nc.scalar.copy(out=out_part[:], in_=acc[m, nt][:])
                nc.sync.dma_start(
                    out=out[m * M_TILE : (m + 1) * M_TILE, nt * N_TILE : (nt + 1) * N_TILE],
                    in_=out_part[:],
                )

        for k in range(AHEAD):
            load_chunk(k)
        square(0)
        for k in range(CHUNKS):
            if k + AHEAD < CHUNKS:
                load_chunk(k + AHEAD)
            if k + 1 < CHUNKS:
                square(k + 1)
            else:
                regroup_x(CHUNKS - 1)
            blend_gate(k)
            if k >= 2:
                quantise_x(k - 2, 0)
            gradient(k)
            if k >= 2:
                quantise_x(k - 2, 1)
            if k > PACK:
                quantise_da_and_multiply(0, k - PACK - 1)
            mean_with_i_n(k)
            negative_mean(k)
            if k >= 1:
                regroup_x(k - 1)
            correction(k)
            if k >= PACK:
                add_da(0, k - PACK)
        for piece in (CHUNKS - 2, CHUNKS - 1):
            for half in range(2):
                quantise_x(piece, half)
        quantise_da_and_multiply(0, EARLY - 1)

        todo = [(1, m) for m in range(EARLY)]
        todo += [(c, m) for m in range(EARLY, M_TILES) for c in range(PASSES)]
        for step in range(len(todo) + 1):
            if step < len(todo):
                add_da(*todo[step])
            if step >= 1:
                c, m = todo[step - 1]
                quantise_da_and_multiply(c, m)
                if c == PASSES - 1:
                    store_rows(m)
